import numpy as np
import ml_dtypes

BF16 = ml_dtypes.bfloat16


def bf(x):
    return np.asarray(x, np.float32).astype(BF16)


def f32(x):
    return np.asarray(x, np.float32)


def f64(x):
    return np.asarray(x).astype(np.float64)


def striped(idx):
    return np.tile(idx.reshape(-1, 16).T, (8, 1))


S, D, NB, L, LQ, E, N = 512, 128, 4, 127, 128, 4, 512


def setup_inputs():
    edge = np.random.standard_normal((NB, E, LQ, LQ))
    dg = np.arange(L)
    edge[:, :, dg, dg] = 0.0
    edge[:, E - 1, dg, dg] = 1.0
    mask = (np.random.random((NB, LQ, LQ)) < 0.5).astype(np.float64)
    al = np.arange(LQ)
    mask[:, al, al] = 1.0
    return {"table": bf(np.random.standard_normal((S, D))), "wv": bf(np.random.standard_normal((D, D)) / np.sqrt(D)), "bv": f32(0.1 * np.random.standard_normal((D, 1))), "edge": f32(edge), "mask": f32(mask), "gate_w": f32(0.02 * np.random.standard_normal((1, E))), "gate_b": f32(0.02 + 0.005 * np.random.standard_normal((1, 1))), "wo": bf(np.random.standard_normal((D, D)) / np.sqrt(D)), "bo": f32(0.1 * np.random.standard_normal((D, 1))), "offs": striped(np.random.permutation(S)[:N])}


def reference(table, wv, bv, edge, mask, gate_w, gate_b, wo, bo, offs):
    idx = offs[:16].T.reshape(-1)
    v = f64(wv).T @ f64(table)[idx].T + f64(bv)
    ef, mk = f64(edge), f64(mask)
    ex = mk * np.exp(ef[:, E - 1])
    p = ex / ex.sum(axis=2, keepdims=True)
    h = mk * (np.einsum("e,nert->nrt", f64(gate_w)[0], ef) + f64(gate_b)[0, 0])
    a = p + h
    y = np.einsum("nrt,dnt->dnr", a, v.reshape(D, NB, LQ)).reshape(D, N)
    return f64(wo).T @ y + f64(bo)

@@ -1,0 +1,118 @@
+import concourse.masks as masks
+import concourse.mybir as mybir
+
+F32, BF16, U16 = mybir.dt.float32, mybir.dt.bfloat16, mybir.dt.uint16
+ALU = mybir.AluOpType
+FUNC = mybir.ActivationFunctionType
+AXIS = mybir.AxisListType
+
+P = 128
+NB = 4
+E = 4
+N = NB * P
+FAR_BELOW = 1.0e30
+
+FLOPS = 3 * 2 * P * P * N
+
+
+def tile_leafonlynet_kernel(tc, table, wv, bv, edge, mask, gate_w, gate_b, wo, bo, offs, out):
+    nc = tc.nc
+    with (
+        tc.tile_pool(name="held", bufs=1) as held,
+        tc.psum_pool(name="psum", bufs=1) as psum,
+    ):
+        offsets = held.tile([P, N // 16], U16, name="offsets")
+        nc.sync.dma_start(offsets[:], offs)
+        tokens = held.tile([P, NB, P], BF16, name="tokens")
+        nc.sync.dma_start(tokens[:], table.rearrange("(k p) c -> p k c", p=P))
+        mask_sb = held.tile([P, NB, P], F32, name="mask_sb")
+        nc.sync.dma_start(mask_sb[:], mask.rearrange("n r t -> r n t"))
+        edge_by_channel = edge.rearrange("n e r t -> e r n t")
+        edge_sb = [held.tile([P, NB, P], F32, name=f"edge{e}") for e in range(E)]
+        for e in (E - 1, 0, 1, 2):
+            nc.sync.dma_start(edge_sb[e][:], edge_by_channel[e])
+
+        wv_sb = held.tile([P, P], BF16, name="wv_sb")
+        nc.scalar.dma_start(wv_sb[:], wv)
+        bv_sb = held.tile([P, 1], F32, name="bv_sb")
+        nc.scalar.dma_start(bv_sb[:], bv)
+        gate_w_sb = held.tile([P, E], F32, name="gate_w_sb")
+        nc.scalar.dma_start(gate_w_sb[:], gate_w.partition_broadcast(P))
+        gate_b_sb = held.tile([P, 1], F32, name="gate_b_sb")
+        nc.scalar.dma_start(gate_b_sb[:], gate_b.partition_broadcast(P))
+        wo_sb = held.tile([P, P], BF16, name="wo_sb")
+        nc.scalar.dma_start(wo_sb[:], wo)
+        bo_sb = held.tile([P, 1], F32, name="bo_sb")
+        nc.scalar.dma_start(bo_sb[:], bo)
+
+        warm = held.tile([P, 1], F32, name="warm")
+        nc.vector.memset(warm[:], 0.0)
+        nc.scalar.activation(warm[:], warm[:], FUNC.Exp)
+
+        identity = held.tile([P, P], BF16, name="identity")
+        masks.make_identity(nc, identity[:])
+
+        table_t_ps = psum.tile([P, N], BF16, name="table_t_ps")
+        for k in range(NB):
+            nc.tensor.transpose(table_t_ps[:, k * P : (k + 1) * P], tokens[:, k, :], identity[:])
+        table_t = held.tile([P, N], BF16, name="table_t")
+        nc.scalar.copy(table_t[:], table_t_ps[:])
+
+        v_ps = psum.tile([P, N], F32, name="v_ps")
+        nc.tensor.matmul(v_ps[:], wv_sb[:], table_t[:].indirect(offsets[:]), start=True, stop=True)
+        v_bf = held.tile([P, N], BF16, name="v_bf")
+        nc.scalar.activation(v_bf[:], v_ps[:], FUNC.Identity, bias=bv_sb[:])
+
+        v_t_ps = psum.tile([P, NB, P], BF16, name="v_t_ps")
+        for n in range(NB):
+            nc.tensor.transpose(v_t_ps[:, n, :], v_bf[:, n * P : (n + 1) * P], identity[:])
+        v_t = held.tile([P, NB, P], BF16, name="v_t")
+        nc.scalar.copy(v_t[:], v_t_ps[:])
+
+        penalty = held.tile([P, NB, P], F32, name="penalty")
+        nc.gpsimd.tensor_scalar(penalty[:], mask_sb[:], FAR_BELOW, -FAR_BELOW, ALU.mult, ALU.add)
+        score = held.tile([P, NB, P], F32, name="score")
+        nc.vector.tensor_tensor(score[:], edge_sb[E - 1][:], penalty[:], ALU.add)
+        minus_top = held.tile([P, NB], F32, name="minus_top")
+        nc.vector.tensor_reduce(minus_top[:], score[:], AXIS.X, ALU.max, negate=True)
+        expd = held.tile([P, NB, P], F32, name="expd")
+        total = held.tile([P, NB], F32, name="total")
+        for n in range(NB):
+            nc.scalar.activation(
+                expd[:, n, :], score[:, n, :], FUNC.Exp, bias=minus_top[:, n : n + 1], accum_out=total[:, n : n + 1]
+            )
+        inv_total = held.tile([P, NB], F32, name="inv_total")
+        nc.vector.reciprocal(inv_total[:], total[:])
+
+        gate = held.tile([P, NB, P], F32, name="gate")
+        nc.vector.tensor_scalar(
+            gate[:], edge_sb[E - 1][:], gate_w_sb[:, E - 1 : E], gate_b_sb[:], ALU.mult, ALU.add
+        )
+        for e in range(E - 1):
+            nc.vector.scalar_tensor_tensor(
+                gate[:], edge_sb[e][:], gate_w_sb[:, e : e + 1], gate[:], ALU.mult, ALU.add
+            )
+        nc.vector.tensor_tensor(gate[:], gate[:], mask_sb[:], ALU.mult)
+
+        a_bf = held.tile([P, NB, P], BF16, name="a_bf")
+        for n in range(NB):
+            nc.vector.scalar_tensor_tensor(
+                a_bf[:, n, :], expd[:, n, :], inv_total[:, n : n + 1], gate[:, n, :], ALU.mult, ALU.add
+            )
+        a_t_ps = psum.tile([P, NB, P], BF16, name="a_t_ps")
+        for n in range(NB):
+            nc.tensor.transpose(a_t_ps[:, n, :], a_bf[:, n, :], identity[:])
+        a_t = held.tile([P, NB, P], BF16, name="a_t")
+        nc.vector.tensor_copy(a_t[:], a_t_ps[:])
+
+        y_ps = psum.tile([P, N], F32, name="y_ps")
+        for n in range(NB):
+            nc.tensor.matmul(y_ps[:, n * P : (n + 1) * P], v_t[:, n, :], a_t[:, n, :], start=True, stop=True)
+        y_bf = held.tile([P, N], BF16, name="y_bf")
+        nc.vector.tensor_copy(y_bf[:], y_ps[:])
+
+        out_ps = psum.tile([P, N], F32, name="out_ps")
+        nc.tensor.matmul(out_ps[:], wo_sb[:], y_bf[:], start=True, stop=True)
+        out_sb = held.tile([P, N], F32, name="out_sb")
+        nc.vector.tensor_scalar(out_sb[:], out_ps[:], bo_sb[:], None, ALU.add)
+        nc.sync.dma_start(out, out_sb[:])

@@ -19,8 +19,13 @@ def tile_leafonlynet_kernel(tc, table, wv, bv, edge, mask, gate_w, gate_b, wo, b
     nc = tc.nc
     with (
         tc.tile_pool(name="held", bufs=1) as held,
-        tc.psum_pool(name="psum", bufs=1) as psum,
+        tc.psum_pool(name="psum_early", bufs=1) as psum_early,
+        tc.psum_pool(name="psum_tail", bufs=2) as psum_tail,
     ):
+        warm = held.tile([P, 1], F32, name="warm")
+        nc.vector.memset(warm[:], 0.0)
+        nc.scalar.activation(warm[:], warm[:], FUNC.Exp)
+
         offsets = held.tile([P, N // 16], U16, name="offsets")
         nc.sync.dma_start(offsets[:], offs)
         tokens = held.tile([P, NB, P], BF16, name="tokens")
@@ -32,45 +37,40 @@ def tile_leafonlynet_kernel(tc, table, wv, bv, edge, mask, gate_w, gate_b, wo, b
         for e in (E - 1, 0, 1, 2):
             nc.sync.dma_start(edge_sb[e][:], edge_by_channel[e])
 
-        wv_sb = held.tile([P, P], BF16, name="wv_sb")
-        nc.scalar.dma_start(wv_sb[:], wv)
-        bv_sb = held.tile([P, 1], F32, name="bv_sb")
-        nc.scalar.dma_start(bv_sb[:], bv)
-        gate_w_sb = held.tile([P, E], F32, name="gate_w_sb")
-        nc.scalar.dma_start(gate_w_sb[:], gate_w.partition_broadcast(P))
-        gate_b_sb = held.tile([P, 1], F32, name="gate_b_sb")
-        nc.scalar.dma_start(gate_b_sb[:], gate_b.partition_broadcast(P))
-        wo_sb = held.tile([P, P], BF16, name="wo_sb")
-        nc.scalar.dma_start(wo_sb[:], wo)
-        bo_sb = held.tile([P, 1], F32, name="bo_sb")
-        nc.scalar.dma_start(bo_sb[:], bo)
-
-        warm = held.tile([P, 1], F32, name="warm")
-        nc.vector.memset(warm[:], 0.0)
-        nc.scalar.activation(warm[:], warm[:], FUNC.Exp)
-
         identity = held.tile([P, P], BF16, name="identity")
         masks.make_identity(nc, identity[:])
+        gate_w_sb = held.tile([P, E], F32, name="gate_w_sb")
+        nc.gpsimd.dma_start(gate_w_sb[:], gate_w.partition_broadcast(P))
+        gate_b_sb = held.tile([P, 1], F32, name="gate_b_sb")
+        nc.gpsimd.dma_start(gate_b_sb[:], gate_b.partition_broadcast(P))
+        wv_sb = held.tile([P, P], BF16, name="wv_sb")
+        nc.gpsimd.dma_start(wv_sb[:], wv)
+        bv_sb = held.tile([P, 1], F32, name="bv_sb")
+        nc.gpsimd.dma_start(bv_sb[:], bv)
+        wo_sb = held.tile([P, P], BF16, name="wo_sb")
+        nc.gpsimd.dma_start(wo_sb[:], wo)
+        bo_sb = held.tile([P, 1], F32, name="bo_sb")
+        nc.gpsimd.dma_start(bo_sb[:], bo)
 
-        table_t_ps = psum.tile([P, N], BF16, name="table_t_ps")
+        table_t_ps = psum_early.tile([P, N], BF16, name="table_t_ps", tag="flipped")
         for k in range(NB):
             nc.tensor.transpose(table_t_ps[:, k * P : (k + 1) * P], tokens[:, k, :], identity[:])
         table_t = held.tile([P, N], BF16, name="table_t")
         nc.scalar.copy(table_t[:], table_t_ps[:])
 
-        v_ps = psum.tile([P, N], F32, name="v_ps")
+        v_ps = psum_early.tile([P, N], F32, name="v_ps")
         nc.tensor.matmul(v_ps[:], wv_sb[:], table_t[:].indirect(offsets[:]), start=True, stop=True)
         v_bf = held.tile([P, N], BF16, name="v_bf")
         nc.scalar.activation(v_bf[:], v_ps[:], FUNC.Identity, bias=bv_sb[:])
 
-        v_t_ps = psum.tile([P, NB, P], BF16, name="v_t_ps")
+        v_t_ps = psum_early.tile([P, N], BF16, name="v_t_ps", tag="flipped")
         for n in range(NB):
-            nc.tensor.transpose(v_t_ps[:, n, :], v_bf[:, n * P : (n + 1) * P], identity[:])
-        v_t = held.tile([P, NB, P], BF16, name="v_t")
+            nc.tensor.transpose(v_t_ps[:, n * P : (n + 1) * P], v_bf[:, n * P : (n + 1) * P], identity[:])
+        v_t = held.tile([P, N], BF16, name="v_t")
         nc.scalar.copy(v_t[:], v_t_ps[:])
 
         penalty = held.tile([P, NB, P], F32, name="penalty")
-        nc.gpsimd.tensor_scalar(penalty[:], mask_sb[:], FAR_BELOW, -FAR_BELOW, ALU.mult, ALU.add)
+        nc.scalar.activation(penalty[:], mask_sb[:], FUNC.Copy, bias=-FAR_BELOW, scale=FAR_BELOW)
         score = held.tile([P, NB, P], F32, name="score")
         nc.vector.tensor_tensor(score[:], edge_sb[E - 1][:], penalty[:], ALU.add)
         minus_top = held.tile([P, NB], F32, name="minus_top")
@@ -85,34 +85,33 @@ def tile_leafonlynet_kernel(tc, table, wv, bv, edge, mask, gate_w, gate_b, wo, b
         nc.vector.reciprocal(inv_total[:], total[:])
 
         gate = held.tile([P, NB, P], F32, name="gate")
-        nc.vector.tensor_scalar(
-            gate[:], edge_sb[E - 1][:], gate_w_sb[:, E - 1 : E], gate_b_sb[:], ALU.mult, ALU.add
+        nc.scalar.activation(
+            gate[:], edge_sb[E - 1][:], FUNC.Identity, bias=gate_b_sb[:], scale=gate_w_sb[:, E - 1 : E]
         )
         for e in range(E - 1):
             nc.vector.scalar_tensor_tensor(
                 gate[:], edge_sb[e][:], gate_w_sb[:, e : e + 1], gate[:], ALU.mult, ALU.add
             )
-        nc.vector.tensor_tensor(gate[:], gate[:], mask_sb[:], ALU.mult)
 
         a_bf = held.tile([P, NB, P], BF16, name="a_bf")
-        for n in range(NB):
-            nc.vector.scalar_tensor_tensor(
-                a_bf[:, n, :], expd[:, n, :], inv_total[:, n : n + 1], gate[:, n, :], ALU.mult, ALU.add
-            )
-        a_t_ps = psum.tile([P, NB, P], BF16, name="a_t_ps")
-        for n in range(NB):
-            nc.tensor.transpose(a_t_ps[:, n, :], a_bf[:, n, :], identity[:])
         a_t = held.tile([P, NB, P], BF16, name="a_t")
-        nc.vector.tensor_copy(a_t[:], a_t_ps[:])
-
-        y_ps = psum.tile([P, N], F32, name="y_ps")
-        for n in range(NB):
-            nc.tensor.matmul(y_ps[:, n * P : (n + 1) * P], v_t[:, n, :], a_t[:, n, :], start=True, stop=True)
-        y_bf = held.tile([P, N], BF16, name="y_bf")
-        nc.vector.tensor_copy(y_bf[:], y_ps[:])
-
-        out_ps = psum.tile([P, N], F32, name="out_ps")
-        nc.tensor.matmul(out_ps[:], wo_sb[:], y_bf[:], start=True, stop=True)
+        y_bf = held.tile([P, NB, P], BF16, name="y_bf")
         out_sb = held.tile([P, N], F32, name="out_sb")
-        nc.vector.tensor_scalar(out_sb[:], out_ps[:], bo_sb[:], None, ALU.add)
-        nc.sync.dma_start(out, out_sb[:])
+        for n in range(NB):
+            block = slice(n * P, (n + 1) * P)
+            nc.vector.scalar_tensor_tensor(
+                gate[:, n, :], expd[:, n, :], inv_total[:, n : n + 1], gate[:, n, :], ALU.mult, ALU.add
+            )
+            nc.vector.tensor_tensor(a_bf[:, n, :], gate[:, n, :], mask_sb[:, n, :], ALU.mult)
+            a_t_ps = psum_tail.tile([P, P], BF16, name="a_t_ps")
+            nc.tensor.transpose(a_t_ps[:], a_bf[:, n, :], identity[:])
+            nc.scalar.copy(a_t[:, n, :], a_t_ps[:])
+            y_ps = psum_tail.tile([P, P], F32, name="y_ps")
+            nc.tensor.matmul(y_ps[:], v_t[:, block], a_t[:, n, :], start=True, stop=True)
+            nc.scalar.copy(y_bf[:, n, :], y_ps[:])
+            out_ps = psum_tail.tile([P, P], F32, name="out_ps")
+            nc.tensor.matmul(out_ps[:], wo_sb[:], y_bf[:, n, :], start=True, stop=True)
+            nc.vector.tensor_scalar(out_sb[:, block], out_ps[:], bo_sb[:], None, ALU.add)
+            if n % 2 == 1:
+                pair = slice((n - 1) * P, (n + 1) * P)
+                nc.sync.dma_start(out[:, pair], out_sb[:, pair])

@@ -22,10 +22,6 @@ def tile_leafonlynet_kernel(tc, table, wv, bv, edge, mask, gate_w, gate_b, wo, b
         tc.psum_pool(name="psum_early", bufs=1) as psum_early,
         tc.psum_pool(name="psum_tail", bufs=2) as psum_tail,
     ):
-        warm = held.tile([P, 1], F32, name="warm")
-        nc.vector.memset(warm[:], 0.0)
-        nc.scalar.activation(warm[:], warm[:], FUNC.Exp)
-
         offsets = held.tile([P, N // 16], U16, name="offsets")
         nc.sync.dma_start(offsets[:], offs)
         tokens = held.tile([P, NB, P], BF16, name="tokens")
@@ -37,20 +33,26 @@ def tile_leafonlynet_kernel(tc, table, wv, bv, edge, mask, gate_w, gate_b, wo, b
         for e in (E - 1, 0, 1, 2):
             nc.sync.dma_start(edge_sb[e][:], edge_by_channel[e])
 
+        wo_sb = held.tile([P, P], BF16, name="wo_sb")
+        nc.sync.dma_start(wo_sb[:], wo)
+        bo_sb = held.tile([P, 1], F32, name="bo_sb")
+        nc.sync.dma_start(bo_sb[:], bo)
+
+        gate_w_sb = held.tile([P, E], F32, name="gate_w_sb")
+        nc.scalar.dma_start(gate_w_sb[:], gate_w.partition_broadcast(P))
+        gate_b_sb = held.tile([P, 1], F32, name="gate_b_sb")
+        nc.scalar.dma_start(gate_b_sb[:], gate_b.partition_broadcast(P))
+        wv_sb = held.tile([P, P], BF16, name="wv_sb")
+        nc.scalar.dma_start(wv_sb[:], wv)
+        bv_sb = held.tile([P, 1], F32, name="bv_sb")
+        nc.scalar.dma_start(bv_sb[:], bv)
+
+        warm = held.tile([P, 1], F32, name="warm")
+        nc.vector.memset(warm[:], 0.0)
+        nc.scalar.activation(warm[:], warm[:], FUNC.Exp)
+
         identity = held.tile([P, P], BF16, name="identity")
         masks.make_identity(nc, identity[:])
-        gate_w_sb = held.tile([P, E], F32, name="gate_w_sb")
-        nc.gpsimd.dma_start(gate_w_sb[:], gate_w.partition_broadcast(P))
-        gate_b_sb = held.tile([P, 1], F32, name="gate_b_sb")
-        nc.gpsimd.dma_start(gate_b_sb[:], gate_b.partition_broadcast(P))
-        wv_sb = held.tile([P, P], BF16, name="wv_sb")
-        nc.gpsimd.dma_start(wv_sb[:], wv)
-        bv_sb = held.tile([P, 1], F32, name="bv_sb")
-        nc.gpsimd.dma_start(bv_sb[:], bv)
-        wo_sb = held.tile([P, P], BF16, name="wo_sb")
-        nc.gpsimd.dma_start(wo_sb[:], wo)
-        bo_sb = held.tile([P, 1], F32, name="bo_sb")
-        nc.gpsimd.dma_start(bo_sb[:], bo)
 
         table_t_ps = psum_early.tile([P, N], BF16, name="table_t_ps", tag="flipped")
         for k in range(NB):

@@ -10,6 +10,8 @@ P = 128
 NB = 4
 E = 4
 N = NB * P
+HALVES = 2
+HB = NB // HALVES
 FAR_BELOW = 1.0e30
 
 FLOPS = 3 * 2 * P * P * N
@@ -22,37 +24,58 @@ def tile_leafonlynet_kernel(tc, table, wv, bv, edge, mask, gate_w, gate_b, wo, b
         tc.psum_pool(name="psum_early", bufs=1) as psum_early,
         tc.psum_pool(name="psum_tail", bufs=2) as psum_tail,
     ):
+        warm = held.tile([P, 1], F32, name="warm")
+        nc.vector.memset(warm[:], 0.0)
+        nc.scalar.activation(warm[:], warm[:], FUNC.Exp)
+
         offsets = held.tile([P, N // 16], U16, name="offsets")
         nc.sync.dma_start(offsets[:], offs)
+        wv_sb = held.tile([P, P], BF16, name="wv_sb")
+        nc.sync.dma_start(wv_sb[:], wv)
+        edge_by_channel = edge.rearrange("n e r t -> e r n t")
+        mask_sb = held.tile([P, NB, P], F32, name="mask_sb")
+        edge_sb = [held.tile([P, NB, P], F32, name=f"edge{e}") for e in range(E)]
+        nc.sync.dma_start(mask_sb[:], mask.rearrange("n r t -> r n t"))
+        nc.sync.dma_start(edge_sb[E - 1][:], edge_by_channel[E - 1])
+        gate_w_sb = held.tile([P, E], F32, name="gate_w_sb")
+        nc.sync.dma_start(gate_w_sb[:], gate_w.partition_broadcast(P))
+        gate_b_sb = held.tile([P, 1], F32, name="gate_b_sb")
+        nc.sync.dma_start(gate_b_sb[:], gate_b.partition_broadcast(P))
         tokens = held.tile([P, NB, P], BF16, name="tokens")
         nc.sync.dma_start(tokens[:], table.rearrange("(k p) c -> p k c", p=P))
-        mask_sb = held.tile([P, NB, P], F32, name="mask_sb")
-        nc.sync.dma_start(mask_sb[:], mask.rearrange("n r t -> r n t"))
-        edge_by_channel = edge.rearrange("n e r t -> e r n t")
-        edge_sb = [held.tile([P, NB, P], F32, name=f"edge{e}") for e in range(E)]
-        for e in (E - 1, 0, 1, 2):
+        for e in range(E - 1):
             nc.sync.dma_start(edge_sb[e][:], edge_by_channel[e])
-
+        bv_sb = held.tile([P, 1], F32, name="bv_sb")
+        nc.sync.dma_start(bv_sb[:], bv)
         wo_sb = held.tile([P, P], BF16, name="wo_sb")
         nc.sync.dma_start(wo_sb[:], wo)
         bo_sb = held.tile([P, 1], F32, name="bo_sb")
         nc.sync.dma_start(bo_sb[:], bo)
 
-        gate_w_sb = held.tile([P, E], F32, name="gate_w_sb")
-        nc.scalar.dma_start(gate_w_sb[:], gate_w.partition_broadcast(P))
-        gate_b_sb = held.tile([P, 1], F32, name="gate_b_sb")
-        nc.scalar.dma_start(gate_b_sb[:], gate_b.partition_broadcast(P))
-        wv_sb = held.tile([P, P], BF16, name="wv_sb")
-        nc.scalar.dma_start(wv_sb[:], wv)
-        bv_sb = held.tile([P, 1], F32, name="bv_sb")
-        nc.scalar.dma_start(bv_sb[:], bv)
-
-        warm = held.tile([P, 1], F32, name="warm")
-        nc.vector.memset(warm[:], 0.0)
-        nc.scalar.activation(warm[:], warm[:], FUNC.Exp)
-
         identity = held.tile([P, P], BF16, name="identity")
         masks.make_identity(nc, identity[:])
+
+        penalty = held.tile([P, NB, P], F32, name="penalty")
+        score = held.tile([P, NB, P], F32, name="score")
+        minus_top = held.tile([P, NB], F32, name="minus_top")
+        expd = held.tile([P, NB, P], F32, name="expd")
+        total = held.tile([P, NB], F32, name="total")
+        inv_total = held.tile([P, NB], F32, name="inv_total")
+        gate = held.tile([P, NB, P], F32, name="gate")
+        for h in range(HALVES):
+            blocks = slice(h * HB, (h + 1) * HB)
+            nc.gpsimd.tensor_scalar(penalty[:, blocks, :], mask_sb[:, blocks, :], FAR_BELOW, -FAR_BELOW, ALU.mult, ALU.add)
+            nc.vector.tensor_tensor(score[:, blocks, :], edge_sb[E - 1][:, blocks, :], penalty[:, blocks, :], ALU.add)
+            nc.vector.tensor_reduce(minus_top[:, blocks], score[:, blocks, :], AXIS.X, ALU.max, negate=True)
+            for n in range(h * HB, (h + 1) * HB):
+                nc.scalar.activation(
+                    expd[:, n, :], score[:, n, :], FUNC.Exp, bias=minus_top[:, n : n + 1], accum_out=total[:, n : n + 1]
+                )
+            nc.vector.reciprocal(inv_total[:, blocks], total[:, blocks])
+            nc.scalar.activation(
+                gate[:, blocks, :], edge_sb[E - 1][:, blocks, :], FUNC.Identity,
+                bias=gate_b_sb[:], scale=gate_w_sb[:, E - 1 : E],
+            )
 
         table_t_ps = psum_early.tile([P, N], BF16, name="table_t_ps", tag="flipped")
         for k in range(NB):
@@ -71,26 +94,12 @@ def tile_leafonlynet_kernel(tc, table, wv, bv, edge, mask, gate_w, gate_b, wo, b
         v_t = held.tile([P, N], BF16, name="v_t")
         nc.scalar.copy(v_t[:], v_t_ps[:])
 
-        penalty = held.tile([P, NB, P], F32, name="penalty")
-        nc.scalar.activation(penalty[:], mask_sb[:], FUNC.Copy, bias=-FAR_BELOW, scale=FAR_BELOW)
-        score = held.tile([P, NB, P], F32, name="score")
-        nc.vector.tensor_tensor(score[:], edge_sb[E - 1][:], penalty[:], ALU.add)
-        minus_top = held.tile([P, NB], F32, name="minus_top")
-        nc.vector.tensor_reduce(minus_top[:], score[:], AXIS.X, ALU.max, negate=True)
-        expd = held.tile([P, NB, P], F32, name="expd")
-        total = held.tile([P, NB], F32, name="total")
         for n in range(NB):
-            nc.scalar.activation(
-                expd[:, n, :], score[:, n, :], FUNC.Exp, bias=minus_top[:, n : n + 1], accum_out=total[:, n : n + 1]
+            nc.vector.scalar_tensor_tensor(
+                gate[:, n, :], expd[:, n, :], inv_total[:, n : n + 1], gate[:, n, :], ALU.mult, ALU.add
             )
-        inv_total = held.tile([P, NB], F32, name="inv_total")
-        nc.vector.reciprocal(inv_total[:], total[:])
 
-        gate = held.tile([P, NB, P], F32, name="gate")
-        nc.scalar.activation(
-            gate[:], edge_sb[E - 1][:], FUNC.Identity, bias=gate_b_sb[:], scale=gate_w_sb[:, E - 1 : E]
-        )
-        for e in range(E - 1):
+        for e in (0, 1):
             nc.vector.scalar_tensor_tensor(
                 gate[:], edge_sb[e][:], gate_w_sb[:, e : e + 1], gate[:], ALU.mult, ALU.add
             )
@@ -102,7 +111,7 @@ def tile_leafonlynet_kernel(tc, table, wv, bv, edge, mask, gate_w, gate_b, wo, b
         for n in range(NB):
             block = slice(n * P, (n + 1) * P)
             nc.vector.scalar_tensor_tensor(
-                gate[:, n, :], expd[:, n, :], inv_total[:, n : n + 1], gate[:, n, :], ALU.mult, ALU.add
+                gate[:, n, :], edge_sb[2][:, n, :], gate_w_sb[:, 2:3], gate[:, n, :], ALU.mult, ALU.add
             )
             nc.vector.tensor_tensor(a_bf[:, n, :], gate[:, n, :], mask_sb[:, n, :], ALU.mult)
             a_t_ps = psum_tail.tile([P, P], BF16, name="a_t_ps")
@@ -114,6 +123,4 @@ def tile_leafonlynet_kernel(tc, table, wv, bv, edge, mask, gate_w, gate_b, wo, b
             out_ps = psum_tail.tile([P, P], F32, name="out_ps")
             nc.tensor.matmul(out_ps[:], wo_sb[:], y_bf[:, n, :], start=True, stop=True)
             nc.vector.tensor_scalar(out_sb[:, block], out_ps[:], bo_sb[:], None, ALU.add)
-            if n % 2 == 1:
-                pair = slice((n - 1) * P, (n + 1) * P)
-                nc.sync.dma_start(out[:, pair], out_sb[:, pair])
+            nc.sync.dma_start(out[:, block], out_sb[:, block])

@@ -21,8 +21,7 @@ def tile_leafonlynet_kernel(tc, table, wv, bv, edge, mask, gate_w, gate_b, wo, b
     nc = tc.nc
     with (
         tc.tile_pool(name="held", bufs=1) as held,
-        tc.psum_pool(name="psum_early", bufs=1) as psum_early,
-        tc.psum_pool(name="psum_tail", bufs=2) as psum_tail,
+        tc.psum_pool(name="banks", bufs=1) as banks,
     ):
         warm = held.tile([P, 1], F32, name="warm")
         nc.vector.memset(warm[:], 0.0)
@@ -30,8 +29,6 @@ def tile_leafonlynet_kernel(tc, table, wv, bv, edge, mask, gate_w, gate_b, wo, b
 
         offsets = held.tile([P, N // 16], U16, name="offsets")
         nc.sync.dma_start(offsets[:], offs)
-        wv_sb = held.tile([P, P], BF16, name="wv_sb")
-        nc.sync.dma_start(wv_sb[:], wv)
         edge_by_channel = edge.rearrange("n e r t -> e r n t")
         mask_sb = held.tile([P, NB, P], F32, name="mask_sb")
         edge_sb = [held.tile([P, NB, P], F32, name=f"edge{e}") for e in range(E)]
@@ -43,84 +40,109 @@ def tile_leafonlynet_kernel(tc, table, wv, bv, edge, mask, gate_w, gate_b, wo, b
         nc.sync.dma_start(gate_b_sb[:], gate_b.partition_broadcast(P))
         tokens = held.tile([P, NB, P], BF16, name="tokens")
         nc.sync.dma_start(tokens[:], table.rearrange("(k p) c -> p k c", p=P))
-        for e in range(E - 1):
-            nc.sync.dma_start(edge_sb[e][:], edge_by_channel[e])
+        wv_sb = held.tile([P, P], BF16, name="wv_sb")
+        nc.sync.dma_start(wv_sb[:], wv)
         bv_sb = held.tile([P, 1], F32, name="bv_sb")
         nc.sync.dma_start(bv_sb[:], bv)
+        for e in range(E - 1):
+            nc.sync.dma_start(edge_sb[e][:], edge_by_channel[e])
         wo_sb = held.tile([P, P], BF16, name="wo_sb")
         nc.sync.dma_start(wo_sb[:], wo)
         bo_sb = held.tile([P, 1], F32, name="bo_sb")
         nc.sync.dma_start(bo_sb[:], bo)
 
-        identity = held.tile([P, P], BF16, name="identity")
-        masks.make_identity(nc, identity[:])
+        identity_f = held.tile([P, P], F32, name="identity_f")
+        masks.make_identity(nc, identity_f[:])
+        identity_b = held.tile([P, P], BF16, name="identity_b")
+        masks.make_identity(nc, identity_b[:])
+
+        def add_flipped(n, term, first=False, last=False):
+            nc.tensor.matmul(x_t_ps[n][:], term[:, n, :], identity_f[:], is_transpose=True, start=first, stop=last)
 
         penalty = held.tile([P, NB, P], F32, name="penalty")
+        nc.vector.tensor_scalar(penalty[:], mask_sb[:], FAR_BELOW, -FAR_BELOW, ALU.mult, ALU.add)
+        mask_t_ps = banks.tile([P, N], F32, name="mask_t_ps", tag="bank_a")
+        for n in range(NB):
+            nc.tensor.transpose(mask_t_ps[:, n * P : (n + 1) * P], mask_sb[:, n, :], identity_f[:])
+        mask_t = held.tile([P, N], BF16, name="mask_t")
+        nc.scalar.copy(mask_t[:], mask_t_ps[:])
+
         score = held.tile([P, NB, P], F32, name="score")
         minus_top = held.tile([P, NB], F32, name="minus_top")
         expd = held.tile([P, NB, P], F32, name="expd")
         total = held.tile([P, NB], F32, name="total")
-        inv_total = held.tile([P, NB], F32, name="inv_total")
-        gate = held.tile([P, NB, P], F32, name="gate")
         for h in range(HALVES):
             blocks = slice(h * HB, (h + 1) * HB)
-            nc.gpsimd.tensor_scalar(penalty[:, blocks, :], mask_sb[:, blocks, :], FAR_BELOW, -FAR_BELOW, ALU.mult, ALU.add)
             nc.vector.tensor_tensor(score[:, blocks, :], edge_sb[E - 1][:, blocks, :], penalty[:, blocks, :], ALU.add)
             nc.vector.tensor_reduce(minus_top[:, blocks], score[:, blocks, :], AXIS.X, ALU.max, negate=True)
             for n in range(h * HB, (h + 1) * HB):
                 nc.scalar.activation(
                     expd[:, n, :], score[:, n, :], FUNC.Exp, bias=minus_top[:, n : n + 1], accum_out=total[:, n : n + 1]
                 )
-            nc.vector.reciprocal(inv_total[:, blocks], total[:, blocks])
-            nc.scalar.activation(
-                gate[:, blocks, :], edge_sb[E - 1][:, blocks, :], FUNC.Identity,
-                bias=gate_b_sb[:], scale=gate_w_sb[:, E - 1 : E],
-            )
 
-        table_t_ps = psum_early.tile([P, N], BF16, name="table_t_ps", tag="flipped")
+        table_t_ps = banks.tile([P, N], BF16, name="table_t_ps", tag="bank_b")
         for k in range(NB):
-            nc.tensor.transpose(table_t_ps[:, k * P : (k + 1) * P], tokens[:, k, :], identity[:])
+            nc.tensor.transpose(table_t_ps[:, k * P : (k + 1) * P], tokens[:, k, :], identity_b[:])
         table_t = held.tile([P, N], BF16, name="table_t")
         nc.scalar.copy(table_t[:], table_t_ps[:])
 
-        v_ps = psum_early.tile([P, N], F32, name="v_ps")
+        v_ps = banks.tile([P, N], F32, name="v_ps", tag="bank_c")
         nc.tensor.matmul(v_ps[:], wv_sb[:], table_t[:].indirect(offsets[:]), start=True, stop=True)
+
+        scaled = [held.tile([P, NB, P], F32, name=f"scaled{e}") for e in range(E)]
+        x_t_ps = [banks.tile([P, P], F32, name=f"x_t_ps{n}") for n in range(NB)]
+        nc.vector.tensor_scalar(
+            scaled[E - 1][:], edge_sb[E - 1][:], gate_w_sb[:, E - 1 : E], gate_b_sb[:], ALU.mult, ALU.add
+        )
+        for n in range(NB):
+            add_flipped(n, scaled[E - 1], first=True)
+        nc.scalar.activation(scaled[0][:], edge_sb[0][:], FUNC.Identity, scale=gate_w_sb[:, 0:1])
+        for n in range(NB):
+            add_flipped(n, scaled[0])
+
         v_bf = held.tile([P, N], BF16, name="v_bf")
-        nc.scalar.activation(v_bf[:], v_ps[:], FUNC.Identity, bias=bv_sb[:])
-
-        v_t_ps = psum_early.tile([P, N], BF16, name="v_t_ps", tag="flipped")
-        for n in range(NB):
-            nc.tensor.transpose(v_t_ps[:, n * P : (n + 1) * P], v_bf[:, n * P : (n + 1) * P], identity[:])
         v_t = held.tile([P, N], BF16, name="v_t")
-        nc.scalar.copy(v_t[:], v_t_ps[:])
+        for h in range(HALVES):
+            half = slice(h * HB * P, (h + 1) * HB * P)
+            nc.scalar.activation(v_bf[:, half], v_ps[:, half], FUNC.Identity, bias=bv_sb[:])
+            v_t_ps = banks.tile([P, HB * P], BF16, name="v_t_ps", tag=("bank_d", "bank_b")[h])
+            for i in range(HB):
+                n = h * HB + i
+                nc.tensor.transpose(v_t_ps[:, i * P : (i + 1) * P], v_bf[:, n * P : (n + 1) * P], identity_b[:])
+            nc.scalar.copy(v_t[:, half], v_t_ps[:])
 
+        nc.vector.tensor_scalar(scaled[1][:], edge_sb[1][:], gate_w_sb[:, 1:2], None, ALU.mult)
         for n in range(NB):
-            nc.vector.scalar_tensor_tensor(
-                gate[:, n, :], expd[:, n, :], inv_total[:, n : n + 1], gate[:, n, :], ALU.mult, ALU.add
-            )
+            add_flipped(n, scaled[1])
 
-        for e in (0, 1):
-            nc.vector.scalar_tensor_tensor(
-                gate[:], edge_sb[e][:], gate_w_sb[:, e : e + 1], gate[:], ALU.mult, ALU.add
-            )
+        inv_total = held.tile([P, NB], F32, name="inv_total")
+        nc.vector.reciprocal(inv_total[:], total[:])
+        soft = held.tile([P, NB, P], F32, name="soft")
+        for n in range(NB):
+            nc.vector.tensor_scalar(soft[:, n, :], expd[:, n, :], inv_total[:, n : n + 1], None, ALU.mult)
+            add_flipped(n, soft)
+        for n in range(NB):
+            nc.vector.tensor_scalar(scaled[2][:, n, :], edge_sb[2][:, n, :], gate_w_sb[:, 2:3], None, ALU.mult)
+            add_flipped(n, scaled[2], last=True)
 
-        a_bf = held.tile([P, NB, P], BF16, name="a_bf")
         a_t = held.tile([P, NB, P], BF16, name="a_t")
         y_bf = held.tile([P, NB, P], BF16, name="y_bf")
         out_sb = held.tile([P, N], F32, name="out_sb")
-        for n in range(NB):
-            block = slice(n * P, (n + 1) * P)
-            nc.vector.scalar_tensor_tensor(
-                gate[:, n, :], edge_sb[2][:, n, :], gate_w_sb[:, 2:3], gate[:, n, :], ALU.mult, ALU.add
-            )
-            nc.vector.tensor_tensor(a_bf[:, n, :], gate[:, n, :], mask_sb[:, n, :], ALU.mult)
-            a_t_ps = psum_tail.tile([P, P], BF16, name="a_t_ps")
-            nc.tensor.transpose(a_t_ps[:], a_bf[:, n, :], identity[:])
-            nc.scalar.copy(a_t[:, n, :], a_t_ps[:])
-            y_ps = psum_tail.tile([P, P], F32, name="y_ps")
-            nc.tensor.matmul(y_ps[:], v_t[:, block], a_t[:, n, :], start=True, stop=True)
-            nc.scalar.copy(y_bf[:, n, :], y_ps[:])
-            out_ps = psum_tail.tile([P, P], F32, name="out_ps")
-            nc.tensor.matmul(out_ps[:], wo_sb[:], y_bf[:, n, :], start=True, stop=True)
-            nc.vector.tensor_scalar(out_sb[:, block], out_ps[:], bo_sb[:], None, ALU.add)
-            nc.sync.dma_start(out[:, block], out_sb[:, block])
+        y_ps = [None] * NB
+        out_ps = [None] * NB
+        for step in range(NB + 2):
+            n = step
+            if n < NB:
+                nc.vector.tensor_tensor(a_t[:, n, :], x_t_ps[n][:], mask_t[:, n * P : (n + 1) * P], ALU.mult)
+                y_ps[n] = banks.tile([P, P], F32, name=f"y_ps{n}", tag=("bank_a", "bank_d")[n % 2])
+                nc.tensor.matmul(y_ps[n][:], v_t[:, n * P : (n + 1) * P], a_t[:, n, :], start=True, stop=True)
+            n = step - 1
+            if 0 <= n < NB:
+                nc.scalar.copy(y_bf[:, n, :], y_ps[n][:])
+                out_ps[n] = banks.tile([P, P], F32, name=f"out_ps{n}", tag=("bank_c", "bank_b")[n % 2])
+                nc.tensor.matmul(out_ps[n][:], wo_sb[:], y_bf[:, n, :], start=True, stop=True)
+            n = step - 2
+            if 0 <= n:
+                block = slice(n * P, (n + 1) * P)
+                nc.vector.tensor_scalar(out_sb[:, block], out_ps[n][:], bo_sb[:], None, ALU.add)
+                nc.sync.dma_start(out[:, block], out_sb[:, block])

@@ -44,10 +44,10 @@ def tile_leafonlynet_kernel(tc, table, wv, bv, edge, mask, gate_w, gate_b, wo, b
         nc.sync.dma_start(wv_sb[:], wv)
         bv_sb = held.tile([P, 1], F32, name="bv_sb")
         nc.sync.dma_start(bv_sb[:], bv)
-        for e in range(E - 1):
-            nc.sync.dma_start(edge_sb[e][:], edge_by_channel[e])
         wo_sb = held.tile([P, P], BF16, name="wo_sb")
         nc.sync.dma_start(wo_sb[:], wo)
+        for e in range(E - 1):
+            nc.sync.dma_start(edge_sb[e][:], edge_by_channel[e])
         bo_sb = held.tile([P, 1], F32, name="bo_sb")
         nc.sync.dma_start(bo_sb[:], bo)
 
@@ -101,15 +101,17 @@ def tile_leafonlynet_kernel(tc, table, wv, bv, edge, mask, gate_w, gate_b, wo, b
             add_flipped(n, scaled[0])
 
         v_bf = held.tile([P, N], BF16, name="v_bf")
-        v_t = held.tile([P, N], BF16, name="v_t")
+        u_t = held.tile([P, N], BF16, name="u_t")
         for h in range(HALVES):
             half = slice(h * HB * P, (h + 1) * HB * P)
             nc.scalar.activation(v_bf[:, half], v_ps[:, half], FUNC.Identity, bias=bv_sb[:])
-            v_t_ps = banks.tile([P, HB * P], BF16, name="v_t_ps", tag=("bank_d", "bank_b")[h])
+            u_t_ps = banks.tile([P, HB * P], F32, name="u_t_ps", tag=("bank_d", "bank_b")[h])
             for i in range(HB):
                 n = h * HB + i
-                nc.tensor.transpose(v_t_ps[:, i * P : (i + 1) * P], v_bf[:, n * P : (n + 1) * P], identity_b[:])
-            nc.scalar.copy(v_t[:, half], v_t_ps[:])
+                nc.tensor.matmul(
+                    u_t_ps[:, i * P : (i + 1) * P], v_bf[:, n * P : (n + 1) * P], wo_sb[:], start=True, stop=True
+                )
+            nc.scalar.copy(u_t[:, half], u_t_ps[:])
 
         nc.vector.tensor_scalar(scaled[1][:], edge_sb[1][:], gate_w_sb[:, 1:2], None, ALU.mult)
         for n in range(NB):
@@ -126,22 +128,15 @@ def tile_leafonlynet_kernel(tc, table, wv, bv, edge, mask, gate_w, gate_b, wo, b
             add_flipped(n, scaled[2], last=True)
 
         a_t = held.tile([P, NB, P], BF16, name="a_t")
-        y_bf = held.tile([P, NB, P], BF16, name="y_bf")
         out_sb = held.tile([P, N], F32, name="out_sb")
-        y_ps = [None] * NB
         out_ps = [None] * NB
-        for step in range(NB + 2):
+        for step in range(NB + 1):
             n = step
             if n < NB:
                 nc.vector.tensor_tensor(a_t[:, n, :], x_t_ps[n][:], mask_t[:, n * P : (n + 1) * P], ALU.mult)
-                y_ps[n] = banks.tile([P, P], F32, name=f"y_ps{n}", tag=("bank_a", "bank_d")[n % 2])
-                nc.tensor.matmul(y_ps[n][:], v_t[:, n * P : (n + 1) * P], a_t[:, n, :], start=True, stop=True)
+                out_ps[n] = banks.tile([P, P], F32, name=f"out_ps{n}", tag=("bank_a", "bank_c")[n % 2])
+                nc.tensor.matmul(out_ps[n][:], u_t[:, n * P : (n + 1) * P], a_t[:, n, :], start=True, stop=True)
             n = step - 1
-            if 0 <= n < NB:
-                nc.scalar.copy(y_bf[:, n, :], y_ps[n][:])
-                out_ps[n] = banks.tile([P, P], F32, name=f"out_ps{n}", tag=("bank_c", "bank_b")[n % 2])
-                nc.tensor.matmul(out_ps[n][:], wo_sb[:], y_bf[:, n, :], start=True, stop=True)
-            n = step - 2
             if 0 <= n:
                 block = slice(n * P, (n + 1) * P)
                 nc.vector.tensor_scalar(out_sb[:, block], out_ps[n][:], bo_sb[:], None, ALU.add)

@@ -113,19 +113,19 @@ def tile_leafonlynet_kernel(tc, table, wv, bv, edge, mask, gate_w, gate_b, wo, b
                 )
             nc.scalar.copy(u_t[:, half], u_t_ps[:])
 
-        nc.vector.tensor_scalar(scaled[1][:], edge_sb[1][:], gate_w_sb[:, 1:2], None, ALU.mult)
-        for n in range(NB):
-            add_flipped(n, scaled[1])
-
+        late = scaled[1]
+        nc.vector.tensor_scalar(late[:], edge_sb[1][:], gate_w_sb[:, 1:2], None, ALU.mult)
         inv_total = held.tile([P, NB], F32, name="inv_total")
         nc.vector.reciprocal(inv_total[:], total[:])
-        soft = held.tile([P, NB, P], F32, name="soft")
         for n in range(NB):
-            nc.vector.tensor_scalar(soft[:, n, :], expd[:, n, :], inv_total[:, n : n + 1], None, ALU.mult)
-            add_flipped(n, soft)
+            nc.vector.scalar_tensor_tensor(
+                late[:, n, :], expd[:, n, :], inv_total[:, n : n + 1], late[:, n, :], ALU.mult, ALU.add
+            )
         for n in range(NB):
-            nc.vector.tensor_scalar(scaled[2][:, n, :], edge_sb[2][:, n, :], gate_w_sb[:, 2:3], None, ALU.mult)
-            add_flipped(n, scaled[2], last=True)
+            nc.vector.scalar_tensor_tensor(
+                late[:, n, :], edge_sb[2][:, n, :], gate_w_sb[:, 2:3], late[:, n, :], ALU.mult, ALU.add
+            )
+            add_flipped(n, late, last=True)
 
         a_t = held.tile([P, NB, P], BF16, name="a_t")
         out_sb = held.tile([P, N], F32, name="out_sb")

@@ -61,7 +61,7 @@ def tile_leafonlynet_kernel(tc, table, wv, bv, edge, mask, gate_w, gate_b, wo, b
 
         penalty = held.tile([P, NB, P], F32, name="penalty")
         nc.vector.tensor_scalar(penalty[:], mask_sb[:], FAR_BELOW, -FAR_BELOW, ALU.mult, ALU.add)
-        mask_t_ps = banks.tile([P, N], F32, name="mask_t_ps", tag="bank_a")
+        mask_t_ps = banks.tile([P, N], F32, name="mask_t_ps", tag="bank_0")
         for n in range(NB):
             nc.tensor.transpose(mask_t_ps[:, n * P : (n + 1) * P], mask_sb[:, n, :], identity_f[:])
         mask_t = held.tile([P, N], BF16, name="mask_t")
@@ -80,14 +80,16 @@ def tile_leafonlynet_kernel(tc, table, wv, bv, edge, mask, gate_w, gate_b, wo, b
                     expd[:, n, :], score[:, n, :], FUNC.Exp, bias=minus_top[:, n : n + 1], accum_out=total[:, n : n + 1]
                 )
 
-        table_t_ps = banks.tile([P, N], BF16, name="table_t_ps", tag="bank_b")
+        table_t_ps = banks.tile([P, N], BF16, name="table_t_ps", tag="bank_1")
         for k in range(NB):
             nc.tensor.transpose(table_t_ps[:, k * P : (k + 1) * P], tokens[:, k, :], identity_b[:])
         table_t = held.tile([P, N], BF16, name="table_t")
         nc.scalar.copy(table_t[:], table_t_ps[:])
 
-        v_ps = banks.tile([P, N], F32, name="v_ps", tag="bank_c")
-        nc.tensor.matmul(v_ps[:], wv_sb[:], table_t[:].indirect(offsets[:]), start=True, stop=True)
+        v_ps = [banks.tile([P, P], F32, name=f"v_ps{n}", tag=f"bank_{n}") for n in range(NB)]
+        for n in range(NB):
+            piece = offsets[:, n * (P // 16) : (n + 1) * (P // 16)]
+            nc.tensor.matmul(v_ps[n][:], wv_sb[:], table_t[:].indirect(piece), start=True, stop=True)
 
         scaled = [held.tile([P, NB, P], F32, name=f"scaled{e}") for e in range(E)]
         x_t_ps = [banks.tile([P, P], F32, name=f"x_t_ps{n}") for n in range(NB)]
@@ -102,16 +104,13 @@ def tile_leafonlynet_kernel(tc, table, wv, bv, edge, mask, gate_w, gate_b, wo, b
 
         v_bf = held.tile([P, N], BF16, name="v_bf")
         u_t = held.tile([P, N], BF16, name="u_t")
-        for h in range(HALVES):
-            half = slice(h * HB * P, (h + 1) * HB * P)
-            nc.scalar.activation(v_bf[:, half], v_ps[:, half], FUNC.Identity, bias=bv_sb[:])
-            u_t_ps = banks.tile([P, HB * P], F32, name="u_t_ps", tag=("bank_d", "bank_b")[h])
-            for i in range(HB):
-                n = h * HB + i
-                nc.tensor.matmul(
-                    u_t_ps[:, i * P : (i + 1) * P], v_bf[:, n * P : (n + 1) * P], wo_sb[:], start=True, stop=True
-                )
-            nc.scalar.copy(u_t[:, half], u_t_ps[:])
+        for n in range(NB):
+            nc.scalar.activation(v_bf[:, n * P : (n + 1) * P], v_ps[n][:], FUNC.Identity, bias=bv_sb[:])
+        u_t_ps = [banks.tile([P, P], F32, name=f"u_t_ps{n}", tag=f"bank_{n}") for n in range(NB)]
+        for n in range(NB):
+            nc.tensor.matmul(u_t_ps[n][:], v_bf[:, n * P : (n + 1) * P], wo_sb[:], start=True, stop=True)
+        for n in range(NB):
+            nc.scalar.copy(u_t[:, n * P : (n + 1) * P], u_t_ps[n][:])
 
         late = scaled[1]
         nc.vector.tensor_scalar(late[:], edge_sb[1][:], gate_w_sb[:, 1:2], None, ALU.mult)
@@ -134,7 +133,7 @@ def tile_leafonlynet_kernel(tc, table, wv, bv, edge, mask, gate_w, gate_b, wo, b
             n = step
             if n < NB:
                 nc.vector.tensor_tensor(a_t[:, n, :], x_t_ps[n][:], mask_t[:, n * P : (n + 1) * P], ALU.mult)
-                out_ps[n] = banks.tile([P, P], F32, name=f"out_ps{n}", tag=("bank_a", "bank_c")[n % 2])
+                out_ps[n] = banks.tile([P, P], F32, name=f"out_ps{n}", tag=f"bank_{n}")
                 nc.tensor.matmul(out_ps[n][:], u_t[:, n * P : (n + 1) * P], a_t[:, n, :], start=True, stop=True)
             n = step - 1
             if 0 <= n:

@@ -12,6 +12,7 @@ E = 4
 N = NB * P
 HALVES = 2
 HB = NB // HALVES
+PIECE = P // 16
 FAR_BELOW = 1.0e30
 
 FLOPS = 3 * 2 * P * P * N
@@ -88,19 +89,19 @@ def tile_leafonlynet_kernel(tc, table, wv, bv, edge, mask, gate_w, gate_b, wo, b
 
         v_ps = [banks.tile([P, P], F32, name=f"v_ps{n}", tag=f"bank_{n}") for n in range(NB)]
         for n in range(NB):
-            piece = offsets[:, n * (P // 16) : (n + 1) * (P // 16)]
+            piece = offsets[:, n * PIECE : (n + 1) * PIECE]
             nc.tensor.matmul(v_ps[n][:], wv_sb[:], table_t[:].indirect(piece), start=True, stop=True)
 
-        scaled = [held.tile([P, NB, P], F32, name=f"scaled{e}") for e in range(E)]
+        gate0 = held.tile([P, NB, P], F32, name="gate0")
+        late = held.tile([P, NB, P], F32, name="late")
+        gate3 = held.tile([P, NB, P], F32, name="gate3")
         x_t_ps = [banks.tile([P, P], F32, name=f"x_t_ps{n}") for n in range(NB)]
-        nc.vector.tensor_scalar(
-            scaled[E - 1][:], edge_sb[E - 1][:], gate_w_sb[:, E - 1 : E], gate_b_sb[:], ALU.mult, ALU.add
-        )
+        nc.vector.tensor_scalar(gate3[:], edge_sb[E - 1][:], gate_w_sb[:, E - 1 : E], gate_b_sb[:], ALU.mult, ALU.add)
         for n in range(NB):
-            add_flipped(n, scaled[E - 1], first=True)
-        nc.scalar.activation(scaled[0][:], edge_sb[0][:], FUNC.Identity, scale=gate_w_sb[:, 0:1])
+            add_flipped(n, gate3, first=True)
+        nc.scalar.activation(gate0[:], edge_sb[0][:], FUNC.Identity, scale=gate_w_sb[:, 0:1])
         for n in range(NB):
-            add_flipped(n, scaled[0])
+            add_flipped(n, gate0)
 
         v_bf = held.tile([P, N], BF16, name="v_bf")
         u_t = held.tile([P, N], BF16, name="u_t")
@@ -112,7 +113,6 @@ def tile_leafonlynet_kernel(tc, table, wv, bv, edge, mask, gate_w, gate_b, wo, b
         for n in range(NB):
             nc.scalar.copy(u_t[:, n * P : (n + 1) * P], u_t_ps[n][:])
 
-        late = scaled[1]
         nc.vector.tensor_scalar(late[:], edge_sb[1][:], gate_w_sb[:, 1:2], None, ALU.mult)
         inv_total = held.tile([P, NB], F32, name="inv_total")
         nc.vector.reciprocal(inv_total[:], total[:])

@@ -62,11 +62,6 @@ def tile_leafonlynet_kernel(tc, table, wv, bv, edge, mask, gate_w, gate_b, wo, b
 
         penalty = held.tile([P, NB, P], F32, name="penalty")
         nc.vector.tensor_scalar(penalty[:], mask_sb[:], FAR_BELOW, -FAR_BELOW, ALU.mult, ALU.add)
-        mask_t_ps = banks.tile([P, N], F32, name="mask_t_ps", tag="bank_0")
-        for n in range(NB):
-            nc.tensor.transpose(mask_t_ps[:, n * P : (n + 1) * P], mask_sb[:, n, :], identity_f[:])
-        mask_t = held.tile([P, N], BF16, name="mask_t")
-        nc.scalar.copy(mask_t[:], mask_t_ps[:])
 
         score = held.tile([P, NB, P], F32, name="score")
         minus_top = held.tile([P, NB], F32, name="minus_top")
@@ -87,6 +82,12 @@ def tile_leafonlynet_kernel(tc, table, wv, bv, edge, mask, gate_w, gate_b, wo, b
         table_t = held.tile([P, N], BF16, name="table_t")
         nc.scalar.copy(table_t[:], table_t_ps[:])
 
+        mask_t_ps = banks.tile([P, N], F32, name="mask_t_ps", tag="bank_3")
+        for n in range(NB):
+            nc.tensor.transpose(mask_t_ps[:, n * P : (n + 1) * P], mask_sb[:, n, :], identity_f[:])
+        mask_t = held.tile([P, N], BF16, name="mask_t")
+        nc.scalar.copy(mask_t[:], mask_t_ps[:])
+
         v_ps = [banks.tile([P, P], F32, name=f"v_ps{n}", tag=f"bank_{n}") for n in range(NB)]
         for n in range(NB):
             piece = offsets[:, n * PIECE : (n + 1) * PIECE]
@@ -99,7 +100,7 @@ def tile_leafonlynet_kernel(tc, table, wv, bv, edge, mask, gate_w, gate_b, wo, b
         nc.vector.tensor_scalar(gate3[:], edge_sb[E - 1][:], gate_w_sb[:, E - 1 : E], gate_b_sb[:], ALU.mult, ALU.add)
         for n in range(NB):
             add_flipped(n, gate3, first=True)
-        nc.scalar.activation(gate0[:], edge_sb[0][:], FUNC.Identity, scale=gate_w_sb[:, 0:1])
+        nc.vector.tensor_scalar(gate0[:], edge_sb[0][:], gate_w_sb[:, 0:1], None, ALU.mult)
         for n in range(NB):
             add_flipped(n, gate0)
 

@@ -108,7 +108,7 @@ def tile_leafonlynet_kernel(tc, table, wv, bv, edge, mask, gate_w, gate_b, wo, b
         u_t = held.tile([P, N], BF16, name="u_t")
         for n in range(NB):
             nc.scalar.activation(v_bf[:, n * P : (n + 1) * P], v_ps[n][:], FUNC.Identity, bias=bv_sb[:])
-        u_t_ps = [banks.tile([P, P], F32, name=f"u_t_ps{n}", tag=f"bank_{n}") for n in range(NB)]
+        u_t_ps = [banks.tile([P, P], BF16, name=f"u_t_ps{n}", tag=f"bank_{n}") for n in range(NB)]
         for n in range(NB):
             nc.tensor.matmul(u_t_ps[n][:], v_bf[:, n * P : (n + 1) * P], wo_sb[:], start=True, stop=True)
         for n in range(NB):

@@ -24,10 +24,6 @@ def tile_leafonlynet_kernel(tc, table, wv, bv, edge, mask, gate_w, gate_b, wo, b
         tc.tile_pool(name="held", bufs=1) as held,
         tc.psum_pool(name="banks", bufs=1) as banks,
     ):
-        warm = held.tile([P, 1], F32, name="warm")
-        nc.vector.memset(warm[:], 0.0)
-        nc.scalar.activation(warm[:], warm[:], FUNC.Exp)
-
         offsets = held.tile([P, N // 16], U16, name="offsets")
         nc.sync.dma_start(offsets[:], offs)
         edge_by_channel = edge.rearrange("n e r t -> e r n t")

import concourse.masks as masks
import concourse.mybir as mybir

F32, BF16, U16 = mybir.dt.float32, mybir.dt.bfloat16, mybir.dt.uint16
ALU = mybir.AluOpType
FUNC = mybir.ActivationFunctionType
AXIS = mybir.AxisListType

P = 128
NB = 4
E = 4
N = NB * P
HALVES = 2
HB = NB // HALVES
PIECE = P // 16
FAR_BELOW = 1.0e30

FLOPS = 3 * 2 * P * P * N


def tile_leafonlynet_kernel(tc, table, wv, bv, edge, mask, gate_w, gate_b, wo, bo, offs, out):
    nc = tc.nc
    with (
        tc.tile_pool(name="held", bufs=1) as held,
        tc.psum_pool(name="banks", bufs=1) as banks,
    ):
        offsets = held.tile([P, N // 16], U16, name="offsets")
        nc.sync.dma_start(offsets[:], offs)
        edge_by_channel = edge.rearrange("n e r t -> e r n t")
        mask_sb = held.tile([P, NB, P], F32, name="mask_sb")
        edge_sb = [held.tile([P, NB, P], F32, name=f"edge{e}") for e in range(E)]
        nc.sync.dma_start(mask_sb[:], mask.rearrange("n r t -> r n t"))
        nc.sync.dma_start(edge_sb[E - 1][:], edge_by_channel[E - 1])
        gate_w_sb = held.tile([P, E], F32, name="gate_w_sb")
        nc.sync.dma_start(gate_w_sb[:], gate_w.partition_broadcast(P))
        gate_b_sb = held.tile([P, 1], F32, name="gate_b_sb")
        nc.sync.dma_start(gate_b_sb[:], gate_b.partition_broadcast(P))
        tokens = held.tile([P, NB, P], BF16, name="tokens")
        nc.sync.dma_start(tokens[:], table.rearrange("(k p) c -> p k c", p=P))
        wv_sb = held.tile([P, P], BF16, name="wv_sb")
        nc.sync.dma_start(wv_sb[:], wv)
        bv_sb = held.tile([P, 1], F32, name="bv_sb")
        nc.sync.dma_start(bv_sb[:], bv)
        wo_sb = held.tile([P, P], BF16, name="wo_sb")
        nc.sync.dma_start(wo_sb[:], wo)
        for e in range(E - 1):
            nc.sync.dma_start(edge_sb[e][:], edge_by_channel[e])
        bo_sb = held.tile([P, 1], F32, name="bo_sb")
        nc.sync.dma_start(bo_sb[:], bo)

        identity_f = held.tile([P, P], F32, name="identity_f")
        masks.make_identity(nc, identity_f[:])
        identity_b = held.tile([P, P], BF16, name="identity_b")
        masks.make_identity(nc, identity_b[:])

        def add_flipped(n, term, first=False, last=False):
            nc.tensor.matmul(x_t_ps[n][:], term[:, n, :], identity_f[:], is_transpose=True, start=first, stop=last)

        penalty = held.tile([P, NB, P], F32, name="penalty")
        nc.vector.tensor_scalar(penalty[:], mask_sb[:], FAR_BELOW, -FAR_BELOW, ALU.mult, ALU.add)

        score = held.tile([P, NB, P], F32, name="score")
        minus_top = held.tile([P, NB], F32, name="minus_top")
        expd = held.tile([P, NB, P], F32, name="expd")
        total = held.tile([P, NB], F32, name="total")
        for h in range(HALVES):
            blocks = slice(h * HB, (h + 1) * HB)
            nc.vector.tensor_tensor(score[:, blocks, :], edge_sb[E - 1][:, blocks, :], penalty[:, blocks, :], ALU.add)
            nc.vector.tensor_reduce(minus_top[:, blocks], score[:, blocks, :], AXIS.X, ALU.max, negate=True)
            for n in range(h * HB, (h + 1) * HB):
                nc.scalar.activation(
                    expd[:, n, :], score[:, n, :], FUNC.Exp, bias=minus_top[:, n : n + 1], accum_out=total[:, n : n + 1]
                )

        table_t_ps = banks.tile([P, N], BF16, name="table_t_ps", tag="bank_1")
        for k in range(NB):
            nc.tensor.transpose(table_t_ps[:, k * P : (k + 1) * P], tokens[:, k, :], identity_b[:])
        table_t = held.tile([P, N], BF16, name="table_t")
        nc.scalar.copy(table_t[:], table_t_ps[:])

        mask_t_ps = banks.tile([P, N], F32, name="mask_t_ps", tag="bank_3")
        for n in range(NB):
            nc.tensor.transpose(mask_t_ps[:, n * P : (n + 1) * P], mask_sb[:, n, :], identity_f[:])
        mask_t = held.tile([P, N], BF16, name="mask_t")
        nc.scalar.copy(mask_t[:], mask_t_ps[:])

        v_ps = [banks.tile([P, P], F32, name=f"v_ps{n}", tag=f"bank_{n}") for n in range(NB)]
        for n in range(NB):
            piece = offsets[:, n * PIECE : (n + 1) * PIECE]
            nc.tensor.matmul(v_ps[n][:], wv_sb[:], table_t[:].indirect(piece), start=True, stop=True)

        gate0 = held.tile([P, NB, P], F32, name="gate0")
        late = held.tile([P, NB, P], F32, name="late")
        gate3 = held.tile([P, NB, P], F32, name="gate3")
        x_t_ps = [banks.tile([P, P], F32, name=f"x_t_ps{n}") for n in range(NB)]
        nc.vector.tensor_scalar(gate3[:], edge_sb[E - 1][:], gate_w_sb[:, E - 1 : E], gate_b_sb[:], ALU.mult, ALU.add)
        for n in range(NB):
            add_flipped(n, gate3, first=True)
        nc.vector.tensor_scalar(gate0[:], edge_sb[0][:], gate_w_sb[:, 0:1], None, ALU.mult)
        for n in range(NB):
            add_flipped(n, gate0)

        v_bf = held.tile([P, N], BF16, name="v_bf")
        u_t = held.tile([P, N], BF16, name="u_t")
        for n in range(NB):
            nc.scalar.activation(v_bf[:, n * P : (n + 1) * P], v_ps[n][:], FUNC.Identity, bias=bv_sb[:])
        u_t_ps = [banks.tile([P, P], BF16, name=f"u_t_ps{n}", tag=f"bank_{n}") for n in range(NB)]
        for n in range(NB):
            nc.tensor.matmul(u_t_ps[n][:], v_bf[:, n * P : (n + 1) * P], wo_sb[:], start=True, stop=True)
        for n in range(NB):
            nc.scalar.copy(u_t[:, n * P : (n + 1) * P], u_t_ps[n][:])

        nc.vector.tensor_scalar(late[:], edge_sb[1][:], gate_w_sb[:, 1:2], None, ALU.mult)
        inv_total = held.tile([P, NB], F32, name="inv_total")
        nc.vector.reciprocal(inv_total[:], total[:])
        for n in range(NB):
            nc.vector.scalar_tensor_tensor(
                late[:, n, :], expd[:, n, :], inv_total[:, n : n + 1], late[:, n, :], ALU.mult, ALU.add
            )
        for n in range(NB):
            nc.vector.scalar_tensor_tensor(
                late[:, n, :], edge_sb[2][:, n, :], gate_w_sb[:, 2:3], late[:, n, :], ALU.mult, ALU.add
            )
            add_flipped(n, late, last=True)

        a_t = held.tile([P, NB, P], BF16, name="a_t")
        out_sb = held.tile([P, N], F32, name="out_sb")
        out_ps = [None] * NB
        for step in range(NB + 1):
            n = step
            if n < NB:
                nc.vector.tensor_tensor(a_t[:, n, :], x_t_ps[n][:], mask_t[:, n * P : (n + 1) * P], ALU.mult)
                out_ps[n] = banks.tile([P, P], F32, name=f"out_ps{n}", tag=f"bank_{n}")
                nc.tensor.matmul(out_ps[n][:], u_t[:, n * P : (n + 1) * P], a_t[:, n, :], start=True, stop=True)
            n = step - 1
            if 0 <= n:
                block = slice(n * P, (n + 1) * P)
                nc.vector.tensor_scalar(out_sb[:, block], out_ps[n][:], bo_sb[:], None, ALU.add)
                nc.sync.dma_start(out[:, block], out_sb[:, block])
